import numpy as np
import ml_dtypes


def mxq(x, axis, fmt="e4m3"):
    dtype, down = {"e4m3": (ml_dtypes.float8_e4m3fn, 7), "e5m2": (ml_dtypes.float8_e5m2, 14)}[fmt]
    v = np.moveaxis(np.asarray(x, np.float32).astype(ml_dtypes.bfloat16).astype(np.float64), axis, -1)
    blocks = v.reshape(v.shape[:-1] + (-1, 32))
    amax = np.abs(blocks).max(-1, keepdims=True)
    byte = np.maximum(np.where(amax > 0, np.frexp(amax)[1] - 1 + 127, 0) - down, 1)
    scale = np.exp2(byte - 127.0)
    codes = (blocks / scale).astype(np.float32).astype(dtype).astype(np.float64)
    return np.moveaxis((codes * scale).reshape(v.shape), -1, axis)


WIDE = False


def mx_kscale(k):
    if not WIDE:
        return np.ones(k)
    levels = np.array([10, -10, 5, -5, 0])
    a = np.random.permutation(np.resize(levels, k // 512 * 4)).reshape(k // 512, 4)
    idx = np.arange(k)
    return np.exp2(a[idx // 512, idx % 128 // 32])


BF16 = ml_dtypes.bfloat16


def bf(x):
    return np.asarray(x, np.float32).astype(BF16)


def f64(x):
    return np.asarray(x).astype(np.float64)


B, T, D, NH, N_MLP = 4, 1024, 512, 8, 4096
HD = D // NH
LN_EPS = 1e-6


def layer_norm(v, g, b):
    mu = v.mean(-1, keepdims=True)
    var = np.square(v - mu).mean(-1, keepdims=True)
    return (v - mu) / np.sqrt(var + LN_EPS) * g + b


def setup_inputs():
    s = mx_kscale(D)
    return {"x": bf(np.random.standard_normal((B, T, D)) * 1.5 + np.random.standard_normal((B, T, 1)) * 0.5),
            "W_qkv": bf(np.random.standard_normal((3 * D, D)) / np.sqrt(D) / s),
            "b_qkv": bf(np.random.standard_normal(3 * D) * 0.2),
            "g1": bf((1.0 + 0.1 * np.random.standard_normal(D)) * s),
            "beta1": bf(0.1 * np.random.standard_normal(D) * s)}


def reference(x, W_qkv, b_qkv, g1, beta1):
    h = layer_norm(f64(x), f64(g1), f64(beta1))
    qkv = (mxq(h, 2, "e4m3") @ mxq(f64(W_qkv), 1, "e4m3").T) + f64(b_qkv)
    qkv = qkv.reshape(B, T, 3, NH, HD)
    return qkv[:, :, 0].copy(), qkv[:, :, 1].copy(), qkv[:, :, 2].copy()

@@ -1,0 +1,198 @@
+from contextlib import ExitStack
+
+import concourse.mybir as mybir
+from concourse.masks import make_identity
+
+F32 = mybir.dt.float32
+BF16 = mybir.dt.bfloat16
+U32 = mybir.dt.uint32
+U8 = mybir.dt.uint8
+FP8X4 = mybir.dt.float8_e4m3fn_x4
+ACT = mybir.ActivationFunctionType
+ALU = mybir.AluOpType
+
+P = 128
+PACK = 4
+D = P * PACK
+TOKENS = 4 * 1024
+OUTS = 3
+ROWS = 4
+GROUP = P * ROWS
+N_GROUPS = TOKENS // GROUP
+W_TILES = OUTS * D // P
+LN_EPS = 1e-6
+
+FLOPS = 2 * TOKENS * D * OUTS * D
+
+
+def tile_block_pa_t_kernel(tc, x, W_qkv, b_qkv, g1, beta1, out_0, out_1, out_2):
+    nc = tc.nc
+
+    x_groups = x.flatten_outer_dims().rearrange("(s p i) k -> s p i k", p=P, i=ROWS)
+    out_groups = [
+        out.rearrange("b t h d -> (b t) (h d)").rearrange("(s p i) f -> s p i f", p=P, i=ROWS)
+        for out in (out_0, out_1, out_2)
+    ]
+    w_rows = W_qkv.rearrange("(r p) k -> p r k", p=P)
+
+    with ExitStack() as ctx:
+        consts = ctx.enter_context(tc.tile_pool(name="consts", bufs=1))
+        x_pool = ctx.enter_context(tc.tile_pool(name="x_pool", bufs=N_GROUPS))
+        small = ctx.enter_context(tc.tile_pool(name="small", bufs=3))
+        xhat_pool = ctx.enter_context(tc.tile_pool(name="xhat_pool", bufs=3))
+        h_pool = ctx.enter_context(tc.tile_pool(name="h_pool", bufs=2))
+        stage_pool = ctx.enter_context(tc.tile_pool(name="stage_pool", bufs=2 * OUTS))
+        turn_psum = ctx.enter_context(tc.psum_pool(name="turn_psum", bufs=4))
+        acc_psum = ctx.enter_context(tc.psum_pool(name="acc_psum", bufs=4))
+
+        x_tiles = []
+        for s in range(N_GROUPS):
+            x_tiles.append(x_pool.tile([P, ROWS, D], BF16, name="x_grp", tag="x_grp"))
+        w_sb = consts.tile([P, W_TILES, D], BF16)
+        affine_rows = consts.tile([P, P], BF16)
+        nc.vector.memset(affine_rows[:], 0.0)
+        bias = consts.tile([P, OUTS, D], BF16)
+
+        nc.sync.dma_start(out=x_tiles[0][:], in_=x_groups[0])
+        nc.sync.dma_start(out=affine_rows[0:PACK, :], in_=g1.rearrange("(t p) -> t p", p=P))
+        nc.sync.dma_start(out=affine_rows[PACK : 2 * PACK, :], in_=beta1.rearrange("(t p) -> t p", p=P))
+        for o in range(OUTS):
+            tiles_of_o = slice(o * PACK, (o + 1) * PACK)
+            nc.sync.dma_start(out=w_sb[:, tiles_of_o, :], in_=w_rows[:, tiles_of_o, :])
+        for s in range(1, N_GROUPS):
+            nc.sync.dma_start(out=x_tiles[s][:], in_=x_groups[s])
+        nc.scalar.dma_start(out=bias[:].rearrange("p o f -> p (o f)"), in_=b_qkv.partition_broadcast(P))
+
+        ident_f32 = consts.tile([P, P], F32)
+        make_identity(nc, ident_f32[:])
+        ident_bf16 = consts.tile([P, P], BF16)
+        make_identity(nc, ident_bf16[:])
+        eps = consts.tile([P, 1], F32)
+        nc.vector.memset(eps[:], LN_EPS)
+        warm = consts.tile([P, 1], F32)
+        nc.scalar.activation(out=warm[:], in_=eps[:], func=ACT.Sqrt)
+
+        affine_ps = turn_psum.tile([P, P], BF16, tag="turn")
+        nc.tensor.transpose(affine_ps[:], affine_rows[:], ident_bf16[:])
+        affine = consts.tile([P, 2 * PACK], F32)
+        nc.vector.tensor_copy(out=affine[:], in_=affine_ps[:, 0 : 2 * PACK])
+
+        w_grouped = consts.tile([P, OUTS * D, PACK], BF16, align_bytes=64)
+        w_codes = consts.tile([P, OUTS * D], U32, align_bytes=64)
+        w_scales = consts.tile([P, OUTS * D], U8, align_bytes=64)
+
+        def quantise_weights():
+            for r in range(W_TILES):
+                w_turned = turn_psum.tile([P, PACK, P], BF16, tag="turn")
+                for t in range(PACK):
+                    nc.tensor.transpose(w_turned[:, t, :], w_sb[:, r, t * P : (t + 1) * P], ident_bf16[:])
+                dst = w_grouped[:, r * P : (r + 1) * P, :]
+                src = w_turned[:].rearrange("p t f -> p f t")
+                if r % 2 == 0:
+                    nc.vector.tensor_copy(out=dst, in_=src)
+                else:
+                    nc.scalar.copy(out=dst, in_=src)
+            for o in range(OUTS):
+                cols = slice(o * D, (o + 1) * D)
+                nc.vector.quantize_mx(
+                    out=w_codes[:, cols].bitcast(FP8X4),
+                    scales=w_scales[:, cols],
+                    in_=w_grouped[:, cols, :].rearrange("p f t -> p (f t)"),
+                )
+
+        xhat_of = {}
+        h_codes_of = {}
+        h_scales_of = {}
+
+        def normalise(s):
+            x_grp = x_tiles[s]
+            stats = small.tile([P, ROWS, 6], F32)
+            mean_var = small.tile([P, ROWS, 2], F32)
+            for i in range(ROWS):
+                nc.vector.bn_stats(out=stats[:, i, :], in_=x_grp[:, i, :])
+            for i in range(ROWS):
+                nc.vector.bn_aggr(out=mean_var[:, i, :], in_=stats[:, i, :])
+            std = small.tile([P, ROWS], F32)
+            nc.scalar.activation(out=std[:], in_=mean_var[:, :, 1], func=ACT.Sqrt, bias=eps[:, 0:1], scale=1.0)
+            rstd = small.tile([P, ROWS], F32)
+            nc.vector.reciprocal(out=rstd[:], in_=std[:])
+            shift = small.tile([P, ROWS], F32)
+            nc.vector.scalar_tensor_tensor(
+                out=shift[:], in0=mean_var[:, :, 0], scalar=-1.0, in1=rstd[:], op0=ALU.mult, op1=ALU.mult
+            )
+            xhat = xhat_pool.tile([P, ROWS, D], F32)
+            for i in range(ROWS):
+                nc.scalar.activation(
+                    out=xhat[:, i, :],
+                    in_=x_grp[:, i, :],
+                    func=ACT.Identity,
+                    scale=rstd[:, i : i + 1],
+                    bias=shift[:, i : i + 1],
+                )
+            xhat_of[s] = xhat
+
+        def turn_and_quantise(s):
+            xhat = xhat_of.pop(s)
+            h_planes = h_pool.tile([P, PACK, GROUP], BF16)
+            for t in range(PACK):
+                plane = turn_psum.tile([P, GROUP], F32, tag="turn")
+                for i in range(ROWS):
+                    nc.tensor.transpose(
+                        plane[:, i * P : (i + 1) * P], xhat[:, i, t * P : (t + 1) * P], ident_f32[:]
+                    )
+                nc.scalar.activation(
+                    out=h_planes[:, t, :],
+                    in_=plane[:],
+                    func=ACT.Identity,
+                    scale=affine[:, t : t + 1],
+                    bias=affine[:, PACK + t : PACK + t + 1],
+                )
+            h_grouped = h_pool.tile([P, GROUP, PACK], BF16, align_bytes=64)
+            nc.vector.tensor_copy(
+                out=h_grouped[:].rearrange("p (c i) t -> p c t i", i=4),
+                in_=h_planes[:].rearrange("p t (c i) -> p c t i", i=4),
+            )
+            h_codes = h_pool.tile([P, GROUP], U32, align_bytes=64)
+            h_scales = h_pool.tile([P, GROUP], U8, align_bytes=64)
+            nc.vector.quantize_mx(
+                out=h_codes[:].bitcast(FP8X4),
+                scales=h_scales[:],
+                in_=h_grouped[:].rearrange("p c t -> p (c t)"),
+            )
+            h_codes_of[s] = h_codes
+            h_scales_of[s] = h_scales
+
+        def project(s):
+            h_codes = h_codes_of.pop(s)
+            h_scales = h_scales_of.pop(s)
+            for o in range(OUTS):
+                stage = stage_pool.tile([P, ROWS, D], F32)
+                for i in range(ROWS):
+                    acc = acc_psum.tile([P, D], F32)
+                    nc.tensor.matmul_mx(
+                        out=acc[:],
+                        lhsT=h_codes[:, i * P : (i + 1) * P].bitcast(FP8X4),
+                        lhsT_scale=h_scales[:, i * P : (i + 1) * P],
+                        rhs=w_codes[:, o * D : (o + 1) * D].bitcast(FP8X4),
+                        rhs_scale=w_scales[:, o * D : (o + 1) * D],
+                        start=True,
+                        stop=True,
+                    )
+                    if i % 2 == 0:
+                        nc.vector.tensor_tensor(out=stage[:, i, :], in0=acc[:], in1=bias[:, o, :], op=ALU.add)
+                    else:
+                        nc.scalar.copy(out=stage[:, i, :], in_=acc[:])
+                        nc.gpsimd.tensor_tensor(
+                            out=stage[:, i, :], in0=stage[:, i, :], in1=bias[:, o, :], op=ALU.add
+                        )
+                nc.sync.dma_start(out=out_groups[o][s], in_=stage[:])
+
+        normalise(0)
+        quantise_weights()
+        for s in range(1, N_GROUPS + 2):
+            if s - 1 < N_GROUPS:
+                turn_and_quantise(s - 1)
+            if s < N_GROUPS:
+                normalise(s)
+            if s >= 2:
+                project(s - 2)

@@ -178,13 +178,7 @@ def tile_block_pa_t_kernel(tc, x, W_qkv, b_qkv, g1, beta1, out_0, out_1, out_2):
                         start=True,
                         stop=True,
                     )
-                    if i % 2 == 0:
-                        nc.vector.tensor_tensor(out=stage[:, i, :], in0=acc[:], in1=bias[:, o, :], op=ALU.add)
-                    else:
-                        nc.scalar.copy(out=stage[:, i, :], in_=acc[:])
-                        nc.gpsimd.tensor_tensor(
-                            out=stage[:, i, :], in0=stage[:, i, :], in1=bias[:, o, :], op=ALU.add
-                        )
+                    nc.vector.tensor_tensor(out=stage[:, i, :], in0=acc[:], in1=bias[:, o, :], op=ALU.add)
                 nc.sync.dma_start(out=out_groups[o][s], in_=stage[:])
 
         normalise(0)

@@ -22,6 +22,8 @@ N_GROUPS = TOKENS // GROUP
 W_TILES = OUTS * D // P
 LN_EPS = 1e-6
 
+STORE_ROWS = 2
+
 FLOPS = 2 * TOKENS * D * OUTS * D
 
 
@@ -38,12 +40,13 @@ def tile_block_pa_t_kernel(tc, x, W_qkv, b_qkv, g1, beta1, out_0, out_1, out_2):
     with ExitStack() as ctx:
         consts = ctx.enter_context(tc.tile_pool(name="consts", bufs=1))
         x_pool = ctx.enter_context(tc.tile_pool(name="x_pool", bufs=N_GROUPS))
-        small = ctx.enter_context(tc.tile_pool(name="small", bufs=3))
+        small = ctx.enter_context(tc.tile_pool(name="small", bufs=4))
         xhat_pool = ctx.enter_context(tc.tile_pool(name="xhat_pool", bufs=3))
-        h_pool = ctx.enter_context(tc.tile_pool(name="h_pool", bufs=2))
-        stage_pool = ctx.enter_context(tc.tile_pool(name="stage_pool", bufs=2 * OUTS))
-        turn_psum = ctx.enter_context(tc.psum_pool(name="turn_psum", bufs=4))
-        acc_psum = ctx.enter_context(tc.psum_pool(name="acc_psum", bufs=4))
+        plane_pool = ctx.enter_context(tc.tile_pool(name="plane_pool", bufs=3))
+        row_pool = ctx.enter_context(tc.tile_pool(name="row_pool", bufs=2 * ROWS))
+        stage_pool = ctx.enter_context(tc.tile_pool(name="stage_pool", bufs=3))
+        turn_psum = ctx.enter_context(tc.psum_pool(name="turn_psum", bufs=2))
+        acc_psum = ctx.enter_context(tc.psum_pool(name="acc_psum", bufs=2))
 
         x_tiles = []
         for s in range(N_GROUPS):
@@ -53,65 +56,79 @@ def tile_block_pa_t_kernel(tc, x, W_qkv, b_qkv, g1, beta1, out_0, out_1, out_2):
         nc.vector.memset(affine_rows[:], 0.0)
         bias = consts.tile([P, OUTS, D], BF16)
 
-        nc.sync.dma_start(out=x_tiles[0][:], in_=x_groups[0])
-        nc.sync.dma_start(out=affine_rows[0:PACK, :], in_=g1.rearrange("(t p) -> t p", p=P))
-        nc.sync.dma_start(out=affine_rows[PACK : 2 * PACK, :], in_=beta1.rearrange("(t p) -> t p", p=P))
-        for o in range(OUTS):
+        def load_weights(o):
             tiles_of_o = slice(o * PACK, (o + 1) * PACK)
             nc.sync.dma_start(out=w_sb[:, tiles_of_o, :], in_=w_rows[:, tiles_of_o, :])
-        for s in range(1, N_GROUPS):
+
+        nc.sync.dma_start(out=x_tiles[0][:], in_=x_groups[0])
+        load_weights(0)
+        nc.sync.dma_start(out=x_tiles[1][:], in_=x_groups[1])
+        load_weights(1)
+        load_weights(2)
+        for s in range(2, N_GROUPS):
             nc.sync.dma_start(out=x_tiles[s][:], in_=x_groups[s])
+        nc.scalar.dma_start(out=affine_rows[0:PACK, :], in_=g1.rearrange("(t p) -> t p", p=P))
+        nc.scalar.dma_start(out=affine_rows[PACK : 2 * PACK, :], in_=beta1.rearrange("(t p) -> t p", p=P))
         nc.scalar.dma_start(out=bias[:].rearrange("p o f -> p (o f)"), in_=b_qkv.partition_broadcast(P))
 
-        ident_f32 = consts.tile([P, P], F32)
-        make_identity(nc, ident_f32[:])
         ident_bf16 = consts.tile([P, P], BF16)
         make_identity(nc, ident_bf16[:])
+        ident_f32 = consts.tile([P, P], F32)
+        make_identity(nc, ident_f32[:])
         eps = consts.tile([P, 1], F32)
         nc.vector.memset(eps[:], LN_EPS)
         warm = consts.tile([P, 1], F32)
         nc.scalar.activation(out=warm[:], in_=eps[:], func=ACT.Sqrt)
 
-        affine_ps = turn_psum.tile([P, P], BF16, tag="turn")
-        nc.tensor.transpose(affine_ps[:], affine_rows[:], ident_bf16[:])
         affine = consts.tile([P, 2 * PACK], F32)
-        nc.vector.tensor_copy(out=affine[:], in_=affine_ps[:, 0 : 2 * PACK])
+
+        def turn_affine():
+            affine_ps = turn_psum.tile([P, P], BF16, tag="turn")
+            nc.tensor.transpose(affine_ps[:], affine_rows[:], ident_bf16[:])
+            nc.vector.tensor_copy(out=affine[:], in_=affine_ps[:, 0 : 2 * PACK])
 
         w_grouped = consts.tile([P, OUTS * D, PACK], BF16, align_bytes=64)
         w_codes = consts.tile([P, OUTS * D], U32, align_bytes=64)
         w_scales = consts.tile([P, OUTS * D], U8, align_bytes=64)
 
-        def quantise_weights():
-            for r in range(W_TILES):
-                w_turned = turn_psum.tile([P, PACK, P], BF16, tag="turn")
-                for t in range(PACK):
-                    nc.tensor.transpose(w_turned[:, t, :], w_sb[:, r, t * P : (t + 1) * P], ident_bf16[:])
-                dst = w_grouped[:, r * P : (r + 1) * P, :]
-                src = w_turned[:].rearrange("p t f -> p f t")
-                if r % 2 == 0:
-                    nc.vector.tensor_copy(out=dst, in_=src)
-                else:
-                    nc.scalar.copy(out=dst, in_=src)
-            for o in range(OUTS):
-                cols = slice(o * D, (o + 1) * D)
-                nc.vector.quantize_mx(
-                    out=w_codes[:, cols].bitcast(FP8X4),
-                    scales=w_scales[:, cols],
-                    in_=w_grouped[:, cols, :].rearrange("p f t -> p (f t)"),
-                )
+        def turn_weight_tile(r):
+            w_turned = acc_psum.tile([P, PACK, P], BF16, tag="acc_%d" % (r % OUTS))
+            for t in range(PACK):
+                nc.tensor.transpose(w_turned[:, t, :], w_sb[:, r, t * P : (t + 1) * P], ident_bf16[:])
+            dst = w_grouped[:, r * P : (r + 1) * P, :]
+            src = w_turned[:].rearrange("p t f -> p f t")
+            if r % OUTS == 0:
+                nc.scalar.copy(out=dst, in_=src)
+            else:
+                nc.vector.tensor_copy(out=dst, in_=src)
 
+        def quantise_weights(o):
+            cols = slice(o * D, (o + 1) * D)
+            nc.vector.quantize_mx(
+                out=w_codes[:, cols].bitcast(FP8X4),
+                scales=w_scales[:, cols],
+                in_=w_grouped[:, cols, :].rearrange("p f t -> p (f t)"),
+            )
+
+        mean_var_of = {}
+        rstd_of = {}
+        shift_of = {}
         xhat_of = {}
-        h_codes_of = {}
-        h_scales_of = {}
+        planes_of = {}
+        grouped_of = {}
+        codes_of = {}
+        scales_of = {}
+        stage_of = {}
 
-        def normalise(s):
-            x_grp = x_tiles[s]
-            stats = small.tile([P, ROWS, 6], F32)
-            mean_var = small.tile([P, ROWS, 2], F32)
-            for i in range(ROWS):
-                nc.vector.bn_stats(out=stats[:, i, :], in_=x_grp[:, i, :])
-            for i in range(ROWS):
-                nc.vector.bn_aggr(out=mean_var[:, i, :], in_=stats[:, i, :])
+        def statistics(s, i):
+            if i == 0:
+                mean_var_of[s] = small.tile([P, ROWS, 2], F32, name="mean_var")
+            stats = small.tile([P, 6], F32)
+            nc.vector.bn_stats(out=stats[:], in_=x_tiles[s][:, i, :])
+            nc.vector.bn_aggr(out=mean_var_of[s][:, i, :], in_=stats[:])
+
+        def finish_statistics(s):
+            mean_var = mean_var_of[s]
             std = small.tile([P, ROWS], F32)
             nc.scalar.activation(out=std[:], in_=mean_var[:, :, 1], func=ACT.Sqrt, bias=eps[:, 0:1], scale=1.0)
             rstd = small.tile([P, ROWS], F32)
@@ -120,73 +137,110 @@ def tile_block_pa_t_kernel(tc, x, W_qkv, b_qkv, g1, beta1, out_0, out_1, out_2):
             nc.vector.scalar_tensor_tensor(
                 out=shift[:], in0=mean_var[:, :, 0], scalar=-1.0, in1=rstd[:], op0=ALU.mult, op1=ALU.mult
             )
-            xhat = xhat_pool.tile([P, ROWS, D], F32)
+            rstd_of[s] = rstd
+            shift_of[s] = shift
+
+        def normalise_row(s, i):
+            if i == 0:
+                xhat_of[s] = xhat_pool.tile([P, ROWS, D], F32, name="xhat")
+            nc.scalar.activation(
+                out=xhat_of[s][:, i, :],
+                in_=x_tiles[s][:, i, :],
+                func=ACT.Identity,
+                scale=rstd_of[s][:, i : i + 1],
+                bias=shift_of[s][:, i : i + 1],
+            )
+
+        def turn_plane(s, t):
+            if t == 0:
+                planes_of[s] = plane_pool.tile([P, PACK, GROUP], BF16, name="planes")
+            plane = turn_psum.tile([P, GROUP], F32, tag="turn")
             for i in range(ROWS):
-                nc.scalar.activation(
-                    out=xhat[:, i, :],
-                    in_=x_grp[:, i, :],
-                    func=ACT.Identity,
-                    scale=rstd[:, i : i + 1],
-                    bias=shift[:, i : i + 1],
+                nc.tensor.transpose(
+                    plane[:, i * P : (i + 1) * P], xhat_of[s][:, i, t * P : (t + 1) * P], ident_f32[:]
                 )
-            xhat_of[s] = xhat
-
-        def turn_and_quantise(s):
-            xhat = xhat_of.pop(s)
-            h_planes = h_pool.tile([P, PACK, GROUP], BF16)
-            for t in range(PACK):
-                plane = turn_psum.tile([P, GROUP], F32, tag="turn")
-                for i in range(ROWS):
-                    nc.tensor.transpose(
-                        plane[:, i * P : (i + 1) * P], xhat[:, i, t * P : (t + 1) * P], ident_f32[:]
-                    )
-                nc.scalar.activation(
-                    out=h_planes[:, t, :],
-                    in_=plane[:],
-                    func=ACT.Identity,
-                    scale=affine[:, t : t + 1],
-                    bias=affine[:, PACK + t : PACK + t + 1],
-                )
-            h_grouped = h_pool.tile([P, GROUP, PACK], BF16, align_bytes=64)
-            nc.vector.tensor_copy(
-                out=h_grouped[:].rearrange("p (c i) t -> p c t i", i=4),
-                in_=h_planes[:].rearrange("p t (c i) -> p c t i", i=4),
+            nc.scalar.activation(
+                out=planes_of[s][:, t, :],
+                in_=plane[:],
+                func=ACT.Identity,
+                scale=affine[:, t : t + 1],
+                bias=affine[:, PACK + t : PACK + t + 1],
             )
-            h_codes = h_pool.tile([P, GROUP], U32, align_bytes=64)
-            h_scales = h_pool.tile([P, GROUP], U8, align_bytes=64)
+
+        def regroup_row(s, i):
+            grouped = row_pool.tile([P, P, PACK], BF16, align_bytes=64)
+            nc.scalar.copy(
+                out=grouped[:].rearrange("p (c j) t -> p c t j", j=4),
+                in_=planes_of[s][:, :, i * P : (i + 1) * P].rearrange("p t (c j) -> p c t j", j=4),
+            )
+            grouped_of[s, i] = grouped
+
+        def quantise_row(s, i):
+            codes = row_pool.tile([P, P], U32, align_bytes=64)
+            scales = row_pool.tile([P, P], U8, align_bytes=64)
             nc.vector.quantize_mx(
-                out=h_codes[:].bitcast(FP8X4),
-                scales=h_scales[:],
-                in_=h_grouped[:].rearrange("p c t -> p (c t)"),
+                out=codes[:].bitcast(FP8X4),
+                scales=scales[:],
+                in_=grouped_of[s, i][:].rearrange("p c t -> p (c t)"),
             )
-            h_codes_of[s] = h_codes
-            h_scales_of[s] = h_scales
+            codes_of[s, i] = codes
+            scales_of[s, i] = scales
 
-        def project(s):
-            h_codes = h_codes_of.pop(s)
-            h_scales = h_scales_of.pop(s)
+        def project_row(s, i):
+            if i == 0:
+                stage_of[s] = [
+                    stage_pool.tile([P, ROWS, D], F32, name="stage_%d" % o) for o in range(OUTS)
+                ]
+            accs = []
             for o in range(OUTS):
-                stage = stage_pool.tile([P, ROWS, D], F32)
-                for i in range(ROWS):
-                    acc = acc_psum.tile([P, D], F32)
-                    nc.tensor.matmul_mx(
-                        out=acc[:],
-                        lhsT=h_codes[:, i * P : (i + 1) * P].bitcast(FP8X4),
-                        lhsT_scale=h_scales[:, i * P : (i + 1) * P],
-                        rhs=w_codes[:, o * D : (o + 1) * D].bitcast(FP8X4),
-                        rhs_scale=w_scales[:, o * D : (o + 1) * D],
-                        start=True,
-                        stop=True,
-                    )
-                    nc.vector.tensor_tensor(out=stage[:, i, :], in0=acc[:], in1=bias[:, o, :], op=ALU.add)
-                nc.sync.dma_start(out=out_groups[o][s], in_=stage[:])
+                acc = acc_psum.tile([P, D], F32, name="acc_%d" % o)
+                nc.tensor.matmul_mx(
+                    out=acc[:],
+                    lhsT=codes_of[s, i][:].bitcast(FP8X4),
+                    lhsT_scale=scales_of[s, i][:],
+                    rhs=w_codes[:, o * D : (o + 1) * D].bitcast(FP8X4),
+                    rhs_scale=w_scales[:, o * D : (o + 1) * D],
+                    start=True,
+                    stop=True,
+                )
+                accs.append(acc)
+            for o in range(OUTS):
+                dst = stage_of[s][o][:, i, :]
+                if o < OUTS - 1:
+                    nc.vector.tensor_tensor(out=dst, in0=accs[o][:], in1=bias[:, o, :], op=ALU.add)
+                else:
+                    nc.scalar.copy(out=dst, in_=accs[o][:])
+                    nc.gpsimd.tensor_tensor(out=dst, in0=dst, in1=bias[:, o, :], op=ALU.add)
+            if (i + 1) % STORE_ROWS == 0:
+                done = slice(i + 1 - STORE_ROWS, i + 1)
+                for o in range(OUTS):
+                    nc.sync.dma_start(out=out_groups[o][s][:, done, :], in_=stage_of[s][o][:, done, :])
+
+        def normalise(s):
+            for i in range(ROWS):
+                statistics(s, i)
+            finish_statistics(s)
+            for i in range(ROWS):
+                normalise_row(s, i)
+
+        def turn(s):
+            for t in range(PACK):
+                turn_plane(s, t)
+            for i in range(ROWS):
+                regroup_row(s, i)
+                quantise_row(s, i)
 
         normalise(0)
-        quantise_weights()
+        for r in range(W_TILES):
+            turn_weight_tile(r)
+        for o in range(OUTS):
+            quantise_weights(o)
+        turn_affine()
         for s in range(1, N_GROUPS + 2):
+            if s >= 2:
+                for i in range(ROWS):
+                    project_row(s - 2, i)
             if s - 1 < N_GROUPS:
-                turn_and_quantise(s - 1)
+                turn(s - 1)
             if s < N_GROUPS:
                 normalise(s)
-            if s >= 2:
-                project(s - 2)

@@ -19,10 +19,21 @@ OUTS = 3
 ROWS = 4
 GROUP = P * ROWS
 N_GROUPS = TOKENS // GROUP
+N_ROWS = N_GROUPS * ROWS
 W_TILES = OUTS * D // P
 LN_EPS = 1e-6
 
 STORE_ROWS = 2
+
+LAG_RSTD = ROWS
+LAG_XHAT = LAG_RSTD + 1
+LAG_TURN = LAG_XHAT + ROWS
+LAG_PLANE_OUT = LAG_TURN + 1
+LAG_REGROUP = LAG_PLANE_OUT + PACK - 1
+LAG_QUANTISE = LAG_REGROUP + 1
+LAG_MATMUL = LAG_QUANTISE + 1
+LAG_BIAS = LAG_MATMUL + 1
+N_STEPS = N_ROWS + LAG_BIAS
 
 FLOPS = 2 * TOKENS * D * OUTS * D
 
@@ -47,6 +58,7 @@ def tile_block_pa_t_kernel(tc, x, W_qkv, b_qkv, g1, beta1, out_0, out_1, out_2):
         stage_pool = ctx.enter_context(tc.tile_pool(name="stage_pool", bufs=3))
         turn_psum = ctx.enter_context(tc.psum_pool(name="turn_psum", bufs=2))
         acc_psum = ctx.enter_context(tc.psum_pool(name="acc_psum", bufs=2))
+        ctx.enter_context(tc.manual_schedule())
 
         x_tiles = []
         for s in range(N_GROUPS):
@@ -97,7 +109,7 @@ def tile_block_pa_t_kernel(tc, x, W_qkv, b_qkv, g1, beta1, out_0, out_1, out_2):
                 nc.tensor.transpose(w_turned[:, t, :], w_sb[:, r, t * P : (t + 1) * P], ident_bf16[:])
             dst = w_grouped[:, r * P : (r + 1) * P, :]
             src = w_turned[:].rearrange("p t f -> p f t")
-            if r % OUTS == 0:
+            if r < PACK:
                 nc.scalar.copy(out=dst, in_=src)
             else:
                 nc.vector.tensor_copy(out=dst, in_=src)
@@ -114,10 +126,12 @@ def tile_block_pa_t_kernel(tc, x, W_qkv, b_qkv, g1, beta1, out_0, out_1, out_2):
         rstd_of = {}
         shift_of = {}
         xhat_of = {}
+        turned_of = {}
         planes_of = {}
         grouped_of = {}
         codes_of = {}
         scales_of = {}
+        accs_of = {}
         stage_of = {}
 
         def statistics(s, i):
@@ -152,16 +166,19 @@ def tile_block_pa_t_kernel(tc, x, W_qkv, b_qkv, g1, beta1, out_0, out_1, out_2):
             )
 
         def turn_plane(s, t):
-            if t == 0:
-                planes_of[s] = plane_pool.tile([P, PACK, GROUP], BF16, name="planes")
             plane = turn_psum.tile([P, GROUP], F32, tag="turn")
             for i in range(ROWS):
                 nc.tensor.transpose(
                     plane[:, i * P : (i + 1) * P], xhat_of[s][:, i, t * P : (t + 1) * P], ident_f32[:]
                 )
+            turned_of[s, t] = plane
+
+        def plane_out(s, t):
+            if t == 0:
+                planes_of[s] = plane_pool.tile([P, PACK, GROUP], BF16, name="planes")
             nc.scalar.activation(
                 out=planes_of[s][:, t, :],
-                in_=plane[:],
+                in_=turned_of[s, t][:],
                 func=ACT.Identity,
                 scale=affine[:, t : t + 1],
                 bias=affine[:, PACK + t : PACK + t + 1],
@@ -186,11 +203,7 @@ def tile_block_pa_t_kernel(tc, x, W_qkv, b_qkv, g1, beta1, out_0, out_1, out_2):
             codes_of[s, i] = codes
             scales_of[s, i] = scales
 
-        def project_row(s, i):
-            if i == 0:
-                stage_of[s] = [
-                    stage_pool.tile([P, ROWS, D], F32, name="stage_%d" % o) for o in range(OUTS)
-                ]
+        def matmul_row(s, i):
             accs = []
             for o in range(OUTS):
                 acc = acc_psum.tile([P, D], F32, name="acc_%d" % o)
@@ -204,6 +217,14 @@ def tile_block_pa_t_kernel(tc, x, W_qkv, b_qkv, g1, beta1, out_0, out_1, out_2):
                     stop=True,
                 )
                 accs.append(acc)
+            accs_of[s, i] = accs
+
+        def bias_row(s, i):
+            if i == 0:
+                stage_of[s] = [
+                    stage_pool.tile([P, ROWS, D], F32, name="stage_%d" % o) for o in range(OUTS)
+                ]
+            accs = accs_of[s, i]
             for o in range(OUTS):
                 dst = stage_of[s][o][:, i, :]
                 if o < OUTS - 1:
@@ -216,31 +237,36 @@ def tile_block_pa_t_kernel(tc, x, W_qkv, b_qkv, g1, beta1, out_0, out_1, out_2):
                 for o in range(OUTS):
                     nc.sync.dma_start(out=out_groups[o][s][:, done, :], in_=stage_of[s][o][:, done, :])
 
-        def normalise(s):
-            for i in range(ROWS):
-                statistics(s, i)
-            finish_statistics(s)
-            for i in range(ROWS):
-                normalise_row(s, i)
-
-        def turn(s):
-            for t in range(PACK):
-                turn_plane(s, t)
-            for i in range(ROWS):
-                regroup_row(s, i)
-                quantise_row(s, i)
-
-        normalise(0)
-        for r in range(W_TILES):
-            turn_weight_tile(r)
-        for o in range(OUTS):
-            quantise_weights(o)
-        turn_affine()
-        for s in range(1, N_GROUPS + 2):
-            if s >= 2:
-                for i in range(ROWS):
-                    project_row(s - 2, i)
-            if s - 1 < N_GROUPS:
-                turn(s - 1)
-            if s < N_GROUPS:
-                normalise(s)
+        for step in range(N_STEPS):
+            n = step - LAG_RSTD
+            if n % ROWS == 0 and 0 <= n < N_ROWS:
+                finish_statistics(n // ROWS)
+            if step < N_ROWS:
+                statistics(step // ROWS, step % ROWS)
+            n = step - LAG_XHAT
+            if 0 <= n < N_ROWS:
+                normalise_row(n // ROWS, n % ROWS)
+            if step < W_TILES:
+                turn_weight_tile(step)
+            elif step < W_TILES + OUTS:
+                quantise_weights(step - W_TILES)
+            if step == LAG_TURN - 1:
+                turn_affine()
+            n = step - LAG_TURN
+            if 0 <= n < N_ROWS:
+                turn_plane(n // PACK, n % PACK)
+            n = step - LAG_PLANE_OUT
+            if 0 <= n < N_ROWS:
+                plane_out(n // PACK, n % PACK)
+            n = step - LAG_MATMUL
+            if 0 <= n < N_ROWS:
+                matmul_row(n // ROWS, n % ROWS)
+            n = step - LAG_BIAS
+            if 0 <= n < N_ROWS:
+                bias_row(n // ROWS, n % ROWS)
+            n = step - LAG_REGROUP
+            if 0 <= n < N_ROWS:
+                regroup_row(n // ROWS, n % ROWS)
+            n = step - LAG_QUANTISE
+            if 0 <= n < N_ROWS:
+                quantise_row(n // ROWS, n % ROWS)

@@ -13,6 +13,7 @@ ALU = mybir.AluOpType
 
 P = 128
 PACK = 4
+HALVES = 2
 D = P * PACK
 TOKENS = 4 * 1024
 OUTS = 3
@@ -22,7 +23,6 @@ N_GROUPS = TOKENS // GROUP
 N_ROWS = N_GROUPS * ROWS
 W_TILES = OUTS * D // P
 LN_EPS = 1e-6
-
 STORE_ROWS = 2
 
 LAG_RSTD = ROWS
@@ -64,7 +64,7 @@ def tile_block_pa_t_kernel(tc, x, W_qkv, b_qkv, g1, beta1, out_0, out_1, out_2):
         for s in range(N_GROUPS):
             x_tiles.append(x_pool.tile([P, ROWS, D], BF16, name="x_grp", tag="x_grp"))
         w_sb = consts.tile([P, W_TILES, D], BF16)
-        affine_rows = consts.tile([P, P], BF16)
+        affine_rows = consts.tile([P, P], F32)
         nc.vector.memset(affine_rows[:], 0.0)
         bias = consts.tile([P, OUTS, D], BF16)
 
@@ -77,14 +77,18 @@ def tile_block_pa_t_kernel(tc, x, W_qkv, b_qkv, g1, beta1, out_0, out_1, out_2):
         nc.sync.dma_start(out=x_tiles[1][:], in_=x_groups[1])
         load_weights(1)
         load_weights(2)
-        for s in range(2, N_GROUPS):
+        nc.sync.dma_start(
+            out=affine_rows[0:HALVES, :], in_=g1.bitcast(F32).rearrange("(u q) -> u q", q=P)
+        )
+        nc.sync.dma_start(
+            out=affine_rows[HALVES : 2 * HALVES, :], in_=beta1.bitcast(F32).rearrange("(u q) -> u q", q=P)
+        )
+        nc.sync.dma_start(out=x_tiles[2][:], in_=x_groups[2])
+        nc.sync.dma_start(out=x_tiles[3][:], in_=x_groups[3])
+        nc.sync.dma_start(out=bias[:].rearrange("p o f -> p (o f)"), in_=b_qkv.partition_broadcast(P))
+        for s in range(4, N_GROUPS):
             nc.sync.dma_start(out=x_tiles[s][:], in_=x_groups[s])
-        nc.scalar.dma_start(out=affine_rows[0:PACK, :], in_=g1.rearrange("(t p) -> t p", p=P))
-        nc.scalar.dma_start(out=affine_rows[PACK : 2 * PACK, :], in_=beta1.rearrange("(t p) -> t p", p=P))
-        nc.scalar.dma_start(out=bias[:].rearrange("p o f -> p (o f)"), in_=b_qkv.partition_broadcast(P))
 
-        ident_bf16 = consts.tile([P, P], BF16)
-        make_identity(nc, ident_bf16[:])
         ident_f32 = consts.tile([P, P], F32)
         make_identity(nc, ident_f32[:])
         eps = consts.tile([P, 1], F32)
@@ -95,20 +99,24 @@ def tile_block_pa_t_kernel(tc, x, W_qkv, b_qkv, g1, beta1, out_0, out_1, out_2):
         affine = consts.tile([P, 2 * PACK], F32)
 
         def turn_affine():
-            affine_ps = turn_psum.tile([P, P], BF16, tag="turn")
-            nc.tensor.transpose(affine_ps[:], affine_rows[:], ident_bf16[:])
-            nc.vector.tensor_copy(out=affine[:], in_=affine_ps[:, 0 : 2 * PACK])
+            affine_ps = turn_psum.tile([P, P], F32, tag="turn")
+            nc.tensor.transpose(affine_ps[:], affine_rows[:], ident_f32[:])
+            affine_words = consts.tile([P, 2 * HALVES], F32)
+            nc.vector.tensor_copy(out=affine_words[:], in_=affine_ps[:, 0 : 2 * HALVES])
+            nc.vector.tensor_copy(out=affine[:], in_=affine_words[:].bitcast(BF16))
 
+        w_words = w_sb[:].bitcast(F32)
         w_grouped = consts.tile([P, OUTS * D, PACK], BF16, align_bytes=64)
+        w_grouped_words = w_grouped[:].bitcast(F32)
         w_codes = consts.tile([P, OUTS * D], U32, align_bytes=64)
         w_scales = consts.tile([P, OUTS * D], U8, align_bytes=64)
 
         def turn_weight_tile(r):
-            w_turned = acc_psum.tile([P, PACK, P], BF16, tag="acc_%d" % (r % OUTS))
-            for t in range(PACK):
-                nc.tensor.transpose(w_turned[:, t, :], w_sb[:, r, t * P : (t + 1) * P], ident_bf16[:])
-            dst = w_grouped[:, r * P : (r + 1) * P, :]
-            src = w_turned[:].rearrange("p t f -> p f t")
+            w_turned = acc_psum.tile([P, HALVES, P], F32, tag="acc_%d" % (r % OUTS))
+            for u in range(HALVES):
+                nc.tensor.transpose(w_turned[:, u, :], w_words[:, r, u * P : (u + 1) * P], ident_f32[:])
+            dst = w_grouped_words[:, r * P : (r + 1) * P, :]
+            src = w_turned[:].rearrange("p u f -> p f u")
             if r < PACK:
                 nc.scalar.copy(out=dst, in_=src)
             else:
@@ -122,6 +130,7 @@ def tile_block_pa_t_kernel(tc, x, W_qkv, b_qkv, g1, beta1, out_0, out_1, out_2):
                 in_=w_grouped[:, cols, :].rearrange("p f t -> p (f t)"),
             )
 
+        stats_of = {}
         mean_var_of = {}
         rstd_of = {}
         shift_of = {}
@@ -136,30 +145,37 @@ def tile_block_pa_t_kernel(tc, x, W_qkv, b_qkv, g1, beta1, out_0, out_1, out_2):
 
         def statistics(s, i):
             if i == 0:
-                mean_var_of[s] = small.tile([P, ROWS, 2], F32, name="mean_var")
-            stats = small.tile([P, 6], F32)
-            nc.vector.bn_stats(out=stats[:], in_=x_tiles[s][:, i, :])
-            nc.vector.bn_aggr(out=mean_var_of[s][:, i, :], in_=stats[:])
+                stats_of[s] = small.tile([P, ROWS, 6], F32, name="stats")
+            nc.vector.bn_stats(out=stats_of[s][:, i, :], in_=x_tiles[s][:, i, :])
 
-        def finish_statistics(s):
-            mean_var = mean_var_of[s]
+        def mean_and_rstd(s):
+            mean_var = small.tile([P, ROWS, 2], F32)
+            for i in range(ROWS):
+                nc.vector.bn_aggr(out=mean_var[:, i, :], in_=stats_of[s][:, i, :])
             std = small.tile([P, ROWS], F32)
             nc.scalar.activation(out=std[:], in_=mean_var[:, :, 1], func=ACT.Sqrt, bias=eps[:, 0:1], scale=1.0)
             rstd = small.tile([P, ROWS], F32)
             nc.vector.reciprocal(out=rstd[:], in_=std[:])
-            shift = small.tile([P, ROWS], F32)
-            nc.vector.scalar_tensor_tensor(
-                out=shift[:], in0=mean_var[:, :, 0], scalar=-1.0, in1=rstd[:], op0=ALU.mult, op1=ALU.mult
-            )
+            mean_var_of[s] = mean_var
             rstd_of[s] = rstd
-            shift_of[s] = shift
+
+        def shift(s):
+            shift_of[s] = small.tile([P, ROWS], F32, name="shift")
+            nc.vector.scalar_tensor_tensor(
+                out=shift_of[s][:],
+                in0=mean_var_of[s][:, :, 0],
+                scalar=-1.0,
+                in1=rstd_of[s][:],
+                op0=ALU.mult,
+                op1=ALU.mult,
+            )
 
         def normalise_row(s, i):
             if i == 0:
                 xhat_of[s] = xhat_pool.tile([P, ROWS, D], F32, name="xhat")
             nc.scalar.activation(
-                out=xhat_of[s][:, i, :],
-                in_=x_tiles[s][:, i, :],
+                out=xhat_of[s][:, i, :].rearrange("p (u e q) -> p u e q", u=HALVES, e=2),
+                in_=x_tiles[s][:, i, :].rearrange("p (u q e) -> p u e q", u=HALVES, e=2),
                 func=ACT.Identity,
                 scale=rstd_of[s][:, i : i + 1],
                 bias=shift_of[s][:, i : i + 1],
@@ -240,9 +256,11 @@ def tile_block_pa_t_kernel(tc, x, W_qkv, b_qkv, g1, beta1, out_0, out_1, out_2):
         for step in range(N_STEPS):
             n = step - LAG_RSTD
             if n % ROWS == 0 and 0 <= n < N_ROWS:
-                finish_statistics(n // ROWS)
+                mean_and_rstd(n // ROWS)
             if step < N_ROWS:
                 statistics(step // ROWS, step % ROWS)
+            if n % ROWS == 0 and 0 <= n < N_ROWS:
+                shift(n // ROWS)
             n = step - LAG_XHAT
             if 0 <= n < N_ROWS:
                 normalise_row(n // ROWS, n % ROWS)

@@ -132,6 +132,7 @@ def tile_block_pa_t_kernel(tc, x, W_qkv, b_qkv, g1, beta1, out_0, out_1, out_2):
 
         stats_of = {}
         mean_var_of = {}
+        std_of = {}
         rstd_of = {}
         shift_of = {}
         xhat_of = {}
@@ -148,16 +149,18 @@ def tile_block_pa_t_kernel(tc, x, W_qkv, b_qkv, g1, beta1, out_0, out_1, out_2):
                 stats_of[s] = small.tile([P, ROWS, 6], F32, name="stats")
             nc.vector.bn_stats(out=stats_of[s][:, i, :], in_=x_tiles[s][:, i, :])
 
-        def mean_and_rstd(s):
+        def mean_and_std(s):
             mean_var = small.tile([P, ROWS, 2], F32)
             for i in range(ROWS):
                 nc.vector.bn_aggr(out=mean_var[:, i, :], in_=stats_of[s][:, i, :])
             std = small.tile([P, ROWS], F32)
             nc.scalar.activation(out=std[:], in_=mean_var[:, :, 1], func=ACT.Sqrt, bias=eps[:, 0:1], scale=1.0)
-            rstd = small.tile([P, ROWS], F32)
-            nc.vector.reciprocal(out=rstd[:], in_=std[:])
             mean_var_of[s] = mean_var
-            rstd_of[s] = rstd
+            std_of[s] = std
+
+        def reciprocal_std(s):
+            rstd_of[s] = small.tile([P, ROWS], F32, name="rstd")
+            nc.vector.reciprocal(out=rstd_of[s][:], in_=std_of[s][:])
 
         def shift(s):
             shift_of[s] = small.tile([P, ROWS], F32, name="shift")
@@ -173,13 +176,25 @@ def tile_block_pa_t_kernel(tc, x, W_qkv, b_qkv, g1, beta1, out_0, out_1, out_2):
         def normalise_row(s, i):
             if i == 0:
                 xhat_of[s] = xhat_pool.tile([P, ROWS, D], F32, name="xhat")
-            nc.scalar.activation(
-                out=xhat_of[s][:, i, :].rearrange("p (u e q) -> p u e q", u=HALVES, e=2),
-                in_=x_tiles[s][:, i, :].rearrange("p (u q e) -> p u e q", u=HALVES, e=2),
-                func=ACT.Identity,
-                scale=rstd_of[s][:, i : i + 1],
-                bias=shift_of[s][:, i : i + 1],
-            )
+            dst = xhat_of[s][:, i, :].rearrange("p (u e q) -> p u e q", u=HALVES, e=2)
+            src = x_tiles[s][:, i, :].rearrange("p (u q e) -> p u e q", u=HALVES, e=2)
+            if i % 2 == 0:
+                nc.scalar.activation(
+                    out=dst,
+                    in_=src,
+                    func=ACT.Identity,
+                    scale=rstd_of[s][:, i : i + 1],
+                    bias=shift_of[s][:, i : i + 1],
+                )
+            else:
+                nc.gpsimd.tensor_scalar(
+                    out=dst,
+                    in0=src,
+                    scalar1=rstd_of[s][:, i : i + 1],
+                    scalar2=shift_of[s][:, i : i + 1],
+                    op0=ALU.mult,
+                    op1=ALU.add,
+                )
 
         def turn_plane(s, t):
             plane = turn_psum.tile([P, GROUP], F32, tag="turn")
@@ -255,12 +270,13 @@ def tile_block_pa_t_kernel(tc, x, W_qkv, b_qkv, g1, beta1, out_0, out_1, out_2):
 
         for step in range(N_STEPS):
             n = step - LAG_RSTD
-            if n % ROWS == 0 and 0 <= n < N_ROWS:
-                mean_and_rstd(n // ROWS)
+            group_is_counted = n % ROWS == 0 and 0 <= n < N_ROWS
+            if group_is_counted:
+                mean_and_std(n // ROWS)
             if step < N_ROWS:
                 statistics(step // ROWS, step % ROWS)
-            if n % ROWS == 0 and 0 <= n < N_ROWS:
-                shift(n // ROWS)
+            if group_is_counted:
+                reciprocal_std(n // ROWS)
             n = step - LAG_XHAT
             if 0 <= n < N_ROWS:
                 normalise_row(n // ROWS, n % ROWS)
@@ -282,6 +298,8 @@ def tile_block_pa_t_kernel(tc, x, W_qkv, b_qkv, g1, beta1, out_0, out_1, out_2):
             n = step - LAG_BIAS
             if 0 <= n < N_ROWS:
                 bias_row(n // ROWS, n % ROWS)
+            if group_is_counted:
+                shift((step - LAG_RSTD) // ROWS)
             n = step - LAG_REGROUP
             if 0 <= n < N_ROWS:
                 regroup_row(n // ROWS, n % ROWS)

@@ -17,19 +17,21 @@ HALVES = 2
 D = P * PACK
 TOKENS = 4 * 1024
 OUTS = 3
-ROWS = 4
+ROWS = 2
 GROUP = P * ROWS
 N_GROUPS = TOKENS // GROUP
 N_ROWS = N_GROUPS * ROWS
 W_TILES = OUTS * D // P
 LN_EPS = 1e-6
-STORE_ROWS = 2
+PLANES_A_STEP = PACK // ROWS
+LOAD_GROUPS = 2
+W_TILES_A_STEP = 2
 
 LAG_RSTD = ROWS
 LAG_XHAT = LAG_RSTD + 1
 LAG_TURN = LAG_XHAT + ROWS
 LAG_PLANE_OUT = LAG_TURN + 1
-LAG_REGROUP = LAG_PLANE_OUT + PACK - 1
+LAG_REGROUP = LAG_PLANE_OUT + ROWS - 1
 LAG_QUANTISE = LAG_REGROUP + 1
 LAG_MATMUL = LAG_QUANTISE + 1
 LAG_BIAS = LAG_MATMUL + 1
@@ -41,7 +43,7 @@ FLOPS = 2 * TOKENS * D * OUTS * D
 def tile_block_pa_t_kernel(tc, x, W_qkv, b_qkv, g1, beta1, out_0, out_1, out_2):
     nc = tc.nc
 
-    x_groups = x.flatten_outer_dims().rearrange("(s p i) k -> s p i k", p=P, i=ROWS)
+    x_loads = x.flatten_outer_dims().rearrange("(a g p i) k -> a p g i k", g=LOAD_GROUPS, p=P, i=ROWS)
     out_groups = [
         out.rearrange("b t h d -> (b t) (h d)").rearrange("(s p i) f -> s p i f", p=P, i=ROWS)
         for out in (out_0, out_1, out_2)
@@ -50,19 +52,26 @@ def tile_block_pa_t_kernel(tc, x, W_qkv, b_qkv, g1, beta1, out_0, out_1, out_2):
 
     with ExitStack() as ctx:
         consts = ctx.enter_context(tc.tile_pool(name="consts", bufs=1))
-        x_pool = ctx.enter_context(tc.tile_pool(name="x_pool", bufs=N_GROUPS))
-        small = ctx.enter_context(tc.tile_pool(name="small", bufs=4))
-        xhat_pool = ctx.enter_context(tc.tile_pool(name="xhat_pool", bufs=3))
-        plane_pool = ctx.enter_context(tc.tile_pool(name="plane_pool", bufs=3))
-        row_pool = ctx.enter_context(tc.tile_pool(name="row_pool", bufs=2 * ROWS))
-        stage_pool = ctx.enter_context(tc.tile_pool(name="stage_pool", bufs=3))
+        x_pool = ctx.enter_context(tc.tile_pool(name="x_pool", bufs=N_GROUPS // LOAD_GROUPS))
+        small = ctx.enter_context(tc.tile_pool(name="small", bufs=6))
+        xhat_pool = ctx.enter_context(tc.tile_pool(name="xhat_pool", bufs=4))
+        plane_pool = ctx.enter_context(tc.tile_pool(name="plane_pool", bufs=4))
+        row_pool = ctx.enter_context(tc.tile_pool(name="row_pool", bufs=8))
+        stage_pool = ctx.enter_context(tc.tile_pool(name="stage_pool", bufs=6))
         turn_psum = ctx.enter_context(tc.psum_pool(name="turn_psum", bufs=2))
         acc_psum = ctx.enter_context(tc.psum_pool(name="acc_psum", bufs=2))
         ctx.enter_context(tc.manual_schedule())
 
         x_tiles = []
-        for s in range(N_GROUPS):
-            x_tiles.append(x_pool.tile([P, ROWS, D], BF16, name="x_grp", tag="x_grp"))
+        for a in range(N_GROUPS // LOAD_GROUPS):
+            x_tiles.append(x_pool.tile([P, LOAD_GROUPS, ROWS, D], BF16, name="x_load", tag="x_load"))
+
+        def x_row(s, i):
+            return x_tiles[s // LOAD_GROUPS][:, s % LOAD_GROUPS, i, :]
+
+        def load_x(a):
+            nc.sync.dma_start(out=x_tiles[a][:], in_=x_loads[a])
+
         w_sb = consts.tile([P, W_TILES, D], BF16)
         affine_rows = consts.tile([P, P], F32)
         nc.vector.memset(affine_rows[:], 0.0)
@@ -72,9 +81,8 @@ def tile_block_pa_t_kernel(tc, x, W_qkv, b_qkv, g1, beta1, out_0, out_1, out_2):
             tiles_of_o = slice(o * PACK, (o + 1) * PACK)
             nc.sync.dma_start(out=w_sb[:, tiles_of_o, :], in_=w_rows[:, tiles_of_o, :])
 
-        nc.sync.dma_start(out=x_tiles[0][:], in_=x_groups[0])
+        load_x(0)
         load_weights(0)
-        nc.sync.dma_start(out=x_tiles[1][:], in_=x_groups[1])
         load_weights(1)
         load_weights(2)
         nc.sync.dma_start(
@@ -83,11 +91,11 @@ def tile_block_pa_t_kernel(tc, x, W_qkv, b_qkv, g1, beta1, out_0, out_1, out_2):
         nc.sync.dma_start(
             out=affine_rows[HALVES : 2 * HALVES, :], in_=beta1.bitcast(F32).rearrange("(u q) -> u q", q=P)
         )
-        nc.sync.dma_start(out=x_tiles[2][:], in_=x_groups[2])
-        nc.sync.dma_start(out=x_tiles[3][:], in_=x_groups[3])
+        load_x(1)
+        load_x(2)
         nc.sync.dma_start(out=bias[:].rearrange("p o f -> p (o f)"), in_=b_qkv.partition_broadcast(P))
-        for s in range(4, N_GROUPS):
-            nc.sync.dma_start(out=x_tiles[s][:], in_=x_groups[s])
+        for a in range(3, N_GROUPS // LOAD_GROUPS):
+            load_x(a)
 
         ident_f32 = consts.tile([P, P], F32)
         make_identity(nc, ident_f32[:])
@@ -115,12 +123,9 @@ def tile_block_pa_t_kernel(tc, x, W_qkv, b_qkv, g1, beta1, out_0, out_1, out_2):
             w_turned = acc_psum.tile([P, HALVES, P], F32, tag="acc_%d" % (r % OUTS))
             for u in range(HALVES):
                 nc.tensor.transpose(w_turned[:, u, :], w_words[:, r, u * P : (u + 1) * P], ident_f32[:])
-            dst = w_grouped_words[:, r * P : (r + 1) * P, :]
-            src = w_turned[:].rearrange("p u f -> p f u")
-            if r < PACK:
-                nc.scalar.copy(out=dst, in_=src)
-            else:
-                nc.vector.tensor_copy(out=dst, in_=src)
+            nc.scalar.copy(
+                out=w_grouped_words[:, r * P : (r + 1) * P, :], in_=w_turned[:].rearrange("p u f -> p f u")
+            )
 
         def quantise_weights(o):
             cols = slice(o * D, (o + 1) * D)
@@ -147,7 +152,7 @@ def tile_block_pa_t_kernel(tc, x, W_qkv, b_qkv, g1, beta1, out_0, out_1, out_2):
         def statistics(s, i):
             if i == 0:
                 stats_of[s] = small.tile([P, ROWS, 6], F32, name="stats")
-            nc.vector.bn_stats(out=stats_of[s][:, i, :], in_=x_tiles[s][:, i, :])
+            nc.vector.bn_stats(out=stats_of[s][:, i, :], in_=x_row(s, i))
 
         def mean_and_std(s):
             mean_var = small.tile([P, ROWS, 2], F32)
@@ -177,7 +182,7 @@ def tile_block_pa_t_kernel(tc, x, W_qkv, b_qkv, g1, beta1, out_0, out_1, out_2):
             if i == 0:
                 xhat_of[s] = xhat_pool.tile([P, ROWS, D], F32, name="xhat")
             dst = xhat_of[s][:, i, :].rearrange("p (u e q) -> p u e q", u=HALVES, e=2)
-            src = x_tiles[s][:, i, :].rearrange("p (u q e) -> p u e q", u=HALVES, e=2)
+            src = x_row(s, i).rearrange("p (u q e) -> p u e q", u=HALVES, e=2)
             if i % 2 == 0:
                 nc.scalar.activation(
                     out=dst,
@@ -196,24 +201,28 @@ def tile_block_pa_t_kernel(tc, x, W_qkv, b_qkv, g1, beta1, out_0, out_1, out_2):
                     op1=ALU.add,
                 )
 
-        def turn_plane(s, t):
-            plane = turn_psum.tile([P, GROUP], F32, tag="turn")
-            for i in range(ROWS):
-                nc.tensor.transpose(
-                    plane[:, i * P : (i + 1) * P], xhat_of[s][:, i, t * P : (t + 1) * P], ident_f32[:]
-                )
-            turned_of[s, t] = plane
+        def turn_planes(s, j):
+            turned = turn_psum.tile([P, PLANES_A_STEP, GROUP], F32, tag="turn")
+            for a in range(PLANES_A_STEP):
+                t = j * PLANES_A_STEP + a
+                for i in range(ROWS):
+                    nc.tensor.transpose(
+                        turned[:, a, i * P : (i + 1) * P], xhat_of[s][:, i, t * P : (t + 1) * P], ident_f32[:]
+                    )
+            turned_of[s, j] = turned
 
-        def plane_out(s, t):
-            if t == 0:
+        def planes_out(s, j):
+            if j == 0:
                 planes_of[s] = plane_pool.tile([P, PACK, GROUP], BF16, name="planes")
-            nc.scalar.activation(
-                out=planes_of[s][:, t, :],
-                in_=turned_of[s, t][:],
-                func=ACT.Identity,
-                scale=affine[:, t : t + 1],
-                bias=affine[:, PACK + t : PACK + t + 1],
-            )
+            for a in range(PLANES_A_STEP):
+                t = j * PLANES_A_STEP + a
+                nc.scalar.activation(
+                    out=planes_of[s][:, t, :],
+                    in_=turned_of[s, j][:, a, :],
+                    func=ACT.Identity,
+                    scale=affine[:, t : t + 1],
+                    bias=affine[:, PACK + t : PACK + t + 1],
+                )
 
         def regroup_row(s, i):
             grouped = row_pool.tile([P, P, PACK], BF16, align_bytes=64)
@@ -263,10 +272,9 @@ def tile_block_pa_t_kernel(tc, x, W_qkv, b_qkv, g1, beta1, out_0, out_1, out_2):
                 else:
                     nc.scalar.copy(out=dst, in_=accs[o][:])
                     nc.gpsimd.tensor_tensor(out=dst, in0=dst, in1=bias[:, o, :], op=ALU.add)
-            if (i + 1) % STORE_ROWS == 0:
-                done = slice(i + 1 - STORE_ROWS, i + 1)
+            if i == ROWS - 1:
                 for o in range(OUTS):
-                    nc.sync.dma_start(out=out_groups[o][s][:, done, :], in_=stage_of[s][o][:, done, :])
+                    nc.sync.dma_start(out=out_groups[o][s], in_=stage_of[s][o][:])
 
         for step in range(N_STEPS):
             n = step - LAG_RSTD
@@ -280,18 +288,19 @@ def tile_block_pa_t_kernel(tc, x, W_qkv, b_qkv, g1, beta1, out_0, out_1, out_2):
             n = step - LAG_XHAT
             if 0 <= n < N_ROWS:
                 normalise_row(n // ROWS, n % ROWS)
-            if step < W_TILES:
-                turn_weight_tile(step)
-            elif step < W_TILES + OUTS:
-                quantise_weights(step - W_TILES)
+            if step < W_TILES // W_TILES_A_STEP:
+                for r in range(step * W_TILES_A_STEP, (step + 1) * W_TILES_A_STEP):
+                    turn_weight_tile(r)
+            elif step < W_TILES // W_TILES_A_STEP + OUTS:
+                quantise_weights(step - W_TILES // W_TILES_A_STEP)
             if step == LAG_TURN - 1:
                 turn_affine()
             n = step - LAG_TURN
             if 0 <= n < N_ROWS:
-                turn_plane(n // PACK, n % PACK)
+                turn_planes(n // ROWS, n % ROWS)
             n = step - LAG_PLANE_OUT
             if 0 <= n < N_ROWS:
-                plane_out(n // PACK, n % PACK)
+                planes_out(n // ROWS, n % ROWS)
             n = step - LAG_MATMUL
             if 0 <= n < N_ROWS:
                 matmul_row(n // ROWS, n % ROWS)

@@ -17,21 +17,19 @@ HALVES = 2
 D = P * PACK
 TOKENS = 4 * 1024
 OUTS = 3
-ROWS = 2
+ROWS = 4
 GROUP = P * ROWS
 N_GROUPS = TOKENS // GROUP
 N_ROWS = N_GROUPS * ROWS
 W_TILES = OUTS * D // P
 LN_EPS = 1e-6
-PLANES_A_STEP = PACK // ROWS
-LOAD_GROUPS = 2
-W_TILES_A_STEP = 2
+STORE_ROWS = 2
 
 LAG_RSTD = ROWS
 LAG_XHAT = LAG_RSTD + 1
 LAG_TURN = LAG_XHAT + ROWS
 LAG_PLANE_OUT = LAG_TURN + 1
-LAG_REGROUP = LAG_PLANE_OUT + ROWS - 1
+LAG_REGROUP = LAG_PLANE_OUT + PACK - 1
 LAG_QUANTISE = LAG_REGROUP + 1
 LAG_MATMUL = LAG_QUANTISE + 1
 LAG_BIAS = LAG_MATMUL + 1
@@ -43,7 +41,7 @@ FLOPS = 2 * TOKENS * D * OUTS * D
 def tile_block_pa_t_kernel(tc, x, W_qkv, b_qkv, g1, beta1, out_0, out_1, out_2):
     nc = tc.nc
 
-    x_loads = x.flatten_outer_dims().rearrange("(a g p i) k -> a p g i k", g=LOAD_GROUPS, p=P, i=ROWS)
+    x_groups = x.flatten_outer_dims().rearrange("(s p i) k -> s p i k", p=P, i=ROWS)
     out_groups = [
         out.rearrange("b t h d -> (b t) (h d)").rearrange("(s p i) f -> s p i f", p=P, i=ROWS)
         for out in (out_0, out_1, out_2)
@@ -52,26 +50,19 @@ def tile_block_pa_t_kernel(tc, x, W_qkv, b_qkv, g1, beta1, out_0, out_1, out_2):
 
     with ExitStack() as ctx:
         consts = ctx.enter_context(tc.tile_pool(name="consts", bufs=1))
-        x_pool = ctx.enter_context(tc.tile_pool(name="x_pool", bufs=N_GROUPS // LOAD_GROUPS))
-        small = ctx.enter_context(tc.tile_pool(name="small", bufs=6))
-        xhat_pool = ctx.enter_context(tc.tile_pool(name="xhat_pool", bufs=4))
-        plane_pool = ctx.enter_context(tc.tile_pool(name="plane_pool", bufs=4))
-        row_pool = ctx.enter_context(tc.tile_pool(name="row_pool", bufs=8))
-        stage_pool = ctx.enter_context(tc.tile_pool(name="stage_pool", bufs=6))
+        x_pool = ctx.enter_context(tc.tile_pool(name="x_pool", bufs=N_GROUPS))
+        small = ctx.enter_context(tc.tile_pool(name="small", bufs=4))
+        xhat_pool = ctx.enter_context(tc.tile_pool(name="xhat_pool", bufs=3))
+        plane_pool = ctx.enter_context(tc.tile_pool(name="plane_pool", bufs=3))
+        row_pool = ctx.enter_context(tc.tile_pool(name="row_pool", bufs=2 * ROWS))
+        stage_pool = ctx.enter_context(tc.tile_pool(name="stage_pool", bufs=3))
         turn_psum = ctx.enter_context(tc.psum_pool(name="turn_psum", bufs=2))
         acc_psum = ctx.enter_context(tc.psum_pool(name="acc_psum", bufs=2))
         ctx.enter_context(tc.manual_schedule())
 
         x_tiles = []
-        for a in range(N_GROUPS // LOAD_GROUPS):
-            x_tiles.append(x_pool.tile([P, LOAD_GROUPS, ROWS, D], BF16, name="x_load", tag="x_load"))
-
-        def x_row(s, i):
-            return x_tiles[s // LOAD_GROUPS][:, s % LOAD_GROUPS, i, :]
-
-        def load_x(a):
-            nc.sync.dma_start(out=x_tiles[a][:], in_=x_loads[a])
-
+        for s in range(N_GROUPS):
+            x_tiles.append(x_pool.tile([P, ROWS, D], BF16, name="x_grp", tag="x_grp"))
         w_sb = consts.tile([P, W_TILES, D], BF16)
         affine_rows = consts.tile([P, P], F32)
         nc.vector.memset(affine_rows[:], 0.0)
@@ -81,8 +72,9 @@ def tile_block_pa_t_kernel(tc, x, W_qkv, b_qkv, g1, beta1, out_0, out_1, out_2):
             tiles_of_o = slice(o * PACK, (o + 1) * PACK)
             nc.sync.dma_start(out=w_sb[:, tiles_of_o, :], in_=w_rows[:, tiles_of_o, :])
 
-        load_x(0)
+        nc.sync.dma_start(out=x_tiles[0][:], in_=x_groups[0])
         load_weights(0)
+        nc.sync.dma_start(out=x_tiles[1][:], in_=x_groups[1])
         load_weights(1)
         load_weights(2)
         nc.sync.dma_start(
@@ -91,11 +83,11 @@ def tile_block_pa_t_kernel(tc, x, W_qkv, b_qkv, g1, beta1, out_0, out_1, out_2):
         nc.sync.dma_start(
             out=affine_rows[HALVES : 2 * HALVES, :], in_=beta1.bitcast(F32).rearrange("(u q) -> u q", q=P)
         )
-        load_x(1)
-        load_x(2)
+        nc.sync.dma_start(out=x_tiles[2][:], in_=x_groups[2])
+        nc.sync.dma_start(out=x_tiles[3][:], in_=x_groups[3])
         nc.sync.dma_start(out=bias[:].rearrange("p o f -> p (o f)"), in_=b_qkv.partition_broadcast(P))
-        for a in range(3, N_GROUPS // LOAD_GROUPS):
-            load_x(a)
+        for s in range(4, N_GROUPS):
+            nc.sync.dma_start(out=x_tiles[s][:], in_=x_groups[s])
 
         ident_f32 = consts.tile([P, P], F32)
         make_identity(nc, ident_f32[:])
@@ -123,9 +115,12 @@ def tile_block_pa_t_kernel(tc, x, W_qkv, b_qkv, g1, beta1, out_0, out_1, out_2):
             w_turned = acc_psum.tile([P, HALVES, P], F32, tag="acc_%d" % (r % OUTS))
             for u in range(HALVES):
                 nc.tensor.transpose(w_turned[:, u, :], w_words[:, r, u * P : (u + 1) * P], ident_f32[:])
-            nc.scalar.copy(
-                out=w_grouped_words[:, r * P : (r + 1) * P, :], in_=w_turned[:].rearrange("p u f -> p f u")
-            )
+            dst = w_grouped_words[:, r * P : (r + 1) * P, :]
+            src = w_turned[:].rearrange("p u f -> p f u")
+            if r < PACK:
+                nc.scalar.copy(out=dst, in_=src)
+            else:
+                nc.vector.tensor_copy(out=dst, in_=src)
 
         def quantise_weights(o):
             cols = slice(o * D, (o + 1) * D)
@@ -152,7 +147,7 @@ def tile_block_pa_t_kernel(tc, x, W_qkv, b_qkv, g1, beta1, out_0, out_1, out_2):
         def statistics(s, i):
             if i == 0:
                 stats_of[s] = small.tile([P, ROWS, 6], F32, name="stats")
-            nc.vector.bn_stats(out=stats_of[s][:, i, :], in_=x_row(s, i))
+            nc.vector.bn_stats(out=stats_of[s][:, i, :], in_=x_tiles[s][:, i, :])
 
         def mean_and_std(s):
             mean_var = small.tile([P, ROWS, 2], F32)
@@ -182,8 +177,8 @@ def tile_block_pa_t_kernel(tc, x, W_qkv, b_qkv, g1, beta1, out_0, out_1, out_2):
             if i == 0:
                 xhat_of[s] = xhat_pool.tile([P, ROWS, D], F32, name="xhat")
             dst = xhat_of[s][:, i, :].rearrange("p (u e q) -> p u e q", u=HALVES, e=2)
-            src = x_row(s, i).rearrange("p (u q e) -> p u e q", u=HALVES, e=2)
-            if i % 2 == 0:
+            src = x_tiles[s][:, i, :].rearrange("p (u q e) -> p u e q", u=HALVES, e=2)
+            if i == 0:
                 nc.scalar.activation(
                     out=dst,
                     in_=src,
@@ -201,28 +196,24 @@ def tile_block_pa_t_kernel(tc, x, W_qkv, b_qkv, g1, beta1, out_0, out_1, out_2):
                     op1=ALU.add,
                 )
 
-        def turn_planes(s, j):
-            turned = turn_psum.tile([P, PLANES_A_STEP, GROUP], F32, tag="turn")
-            for a in range(PLANES_A_STEP):
-                t = j * PLANES_A_STEP + a
-                for i in range(ROWS):
-                    nc.tensor.transpose(
-                        turned[:, a, i * P : (i + 1) * P], xhat_of[s][:, i, t * P : (t + 1) * P], ident_f32[:]
-                    )
-            turned_of[s, j] = turned
-
-        def planes_out(s, j):
-            if j == 0:
-                planes_of[s] = plane_pool.tile([P, PACK, GROUP], BF16, name="planes")
-            for a in range(PLANES_A_STEP):
-                t = j * PLANES_A_STEP + a
-                nc.scalar.activation(
-                    out=planes_of[s][:, t, :],
-                    in_=turned_of[s, j][:, a, :],
-                    func=ACT.Identity,
-                    scale=affine[:, t : t + 1],
-                    bias=affine[:, PACK + t : PACK + t + 1],
+        def turn_plane(s, t):
+            plane = turn_psum.tile([P, GROUP], F32, tag="turn")
+            for i in range(ROWS):
+                nc.tensor.transpose(
+                    plane[:, i * P : (i + 1) * P], xhat_of[s][:, i, t * P : (t + 1) * P], ident_f32[:]
                 )
+            turned_of[s, t] = plane
+
+        def plane_out(s, t):
+            if t == 0:
+                planes_of[s] = plane_pool.tile([P, PACK, GROUP], BF16, name="planes")
+            nc.scalar.activation(
+                out=planes_of[s][:, t, :],
+                in_=turned_of[s, t][:],
+                func=ACT.Identity,
+                scale=affine[:, t : t + 1],
+                bias=affine[:, PACK + t : PACK + t + 1],
+            )
 
         def regroup_row(s, i):
             grouped = row_pool.tile([P, P, PACK], BF16, align_bytes=64)
@@ -272,9 +263,10 @@ def tile_block_pa_t_kernel(tc, x, W_qkv, b_qkv, g1, beta1, out_0, out_1, out_2):
                 else:
                     nc.scalar.copy(out=dst, in_=accs[o][:])
                     nc.gpsimd.tensor_tensor(out=dst, in0=dst, in1=bias[:, o, :], op=ALU.add)
-            if i == ROWS - 1:
+            if (i + 1) % STORE_ROWS == 0:
+                done = slice(i + 1 - STORE_ROWS, i + 1)
                 for o in range(OUTS):
-                    nc.sync.dma_start(out=out_groups[o][s], in_=stage_of[s][o][:])
+                    nc.sync.dma_start(out=out_groups[o][s][:, done, :], in_=stage_of[s][o][:, done, :])
 
         for step in range(N_STEPS):
             n = step - LAG_RSTD
@@ -288,19 +280,18 @@ def tile_block_pa_t_kernel(tc, x, W_qkv, b_qkv, g1, beta1, out_0, out_1, out_2):
             n = step - LAG_XHAT
             if 0 <= n < N_ROWS:
                 normalise_row(n // ROWS, n % ROWS)
-            if step < W_TILES // W_TILES_A_STEP:
-                for r in range(step * W_TILES_A_STEP, (step + 1) * W_TILES_A_STEP):
-                    turn_weight_tile(r)
-            elif step < W_TILES // W_TILES_A_STEP + OUTS:
-                quantise_weights(step - W_TILES // W_TILES_A_STEP)
+            if step < W_TILES:
+                turn_weight_tile(step)
+            elif step < W_TILES + OUTS:
+                quantise_weights(step - W_TILES)
             if step == LAG_TURN - 1:
                 turn_affine()
             n = step - LAG_TURN
             if 0 <= n < N_ROWS:
-                turn_planes(n // ROWS, n % ROWS)
+                turn_plane(n // PACK, n % PACK)
             n = step - LAG_PLANE_OUT
             if 0 <= n < N_ROWS:
-                planes_out(n // ROWS, n % ROWS)
+                plane_out(n // PACK, n % PACK)
             n = step - LAG_MATMUL
             if 0 <= n < N_ROWS:
                 matmul_row(n // ROWS, n % ROWS)

from contextlib import ExitStack

import concourse.mybir as mybir
from concourse.masks import make_identity

F32 = mybir.dt.float32
BF16 = mybir.dt.bfloat16
U32 = mybir.dt.uint32
U8 = mybir.dt.uint8
FP8X4 = mybir.dt.float8_e4m3fn_x4
ACT = mybir.ActivationFunctionType
ALU = mybir.AluOpType

P = 128
PACK = 4
HALVES = 2
D = P * PACK
TOKENS = 4 * 1024
OUTS = 3
ROWS = 4
GROUP = P * ROWS
N_GROUPS = TOKENS // GROUP
N_ROWS = N_GROUPS * ROWS
W_TILES = OUTS * D // P
LN_EPS = 1e-6
STORE_ROWS = 2

LAG_RSTD = ROWS
LAG_XHAT = LAG_RSTD + 1
LAG_TURN = LAG_XHAT + ROWS
LAG_PLANE_OUT = LAG_TURN + 1
LAG_REGROUP = LAG_PLANE_OUT + PACK - 1
LAG_QUANTISE = LAG_REGROUP + 1
LAG_MATMUL = LAG_QUANTISE + 1
LAG_BIAS = LAG_MATMUL + 1
N_STEPS = N_ROWS + LAG_BIAS

FLOPS = 2 * TOKENS * D * OUTS * D


def tile_block_pa_t_kernel(tc, x, W_qkv, b_qkv, g1, beta1, out_0, out_1, out_2):
    nc = tc.nc

    x_groups = x.flatten_outer_dims().rearrange("(s p i) k -> s p i k", p=P, i=ROWS)
    out_groups = [
        out.rearrange("b t h d -> (b t) (h d)").rearrange("(s p i) f -> s p i f", p=P, i=ROWS)
        for out in (out_0, out_1, out_2)
    ]
    w_rows = W_qkv.rearrange("(r p) k -> p r k", p=P)

    with ExitStack() as ctx:
        consts = ctx.enter_context(tc.tile_pool(name="consts", bufs=1))
        x_pool = ctx.enter_context(tc.tile_pool(name="x_pool", bufs=N_GROUPS))
        small = ctx.enter_context(tc.tile_pool(name="small", bufs=4))
        xhat_pool = ctx.enter_context(tc.tile_pool(name="xhat_pool", bufs=3))
        plane_pool = ctx.enter_context(tc.tile_pool(name="plane_pool", bufs=3))
        row_pool = ctx.enter_context(tc.tile_pool(name="row_pool", bufs=2 * ROWS))
        stage_pool = ctx.enter_context(tc.tile_pool(name="stage_pool", bufs=3))
        turn_psum = ctx.enter_context(tc.psum_pool(name="turn_psum", bufs=2))
        acc_psum = ctx.enter_context(tc.psum_pool(name="acc_psum", bufs=2))
        ctx.enter_context(tc.manual_schedule())

        x_tiles = []
        for s in range(N_GROUPS):
            x_tiles.append(x_pool.tile([P, ROWS, D], BF16, name="x_grp", tag="x_grp"))
        w_sb = consts.tile([P, W_TILES, D], BF16)
        affine_rows = consts.tile([P, P], F32)
        nc.vector.memset(affine_rows[:], 0.0)
        bias = consts.tile([P, OUTS, D], BF16)

        def load_weights(o):
            tiles_of_o = slice(o * PACK, (o + 1) * PACK)
            nc.sync.dma_start(out=w_sb[:, tiles_of_o, :], in_=w_rows[:, tiles_of_o, :])

        nc.sync.dma_start(out=x_tiles[0][:], in_=x_groups[0])
        load_weights(0)
        nc.sync.dma_start(out=x_tiles[1][:], in_=x_groups[1])
        load_weights(1)
        load_weights(2)
        nc.sync.dma_start(
            out=affine_rows[0:HALVES, :], in_=g1.bitcast(F32).rearrange("(u q) -> u q", q=P)
        )
        nc.sync.dma_start(
            out=affine_rows[HALVES : 2 * HALVES, :], in_=beta1.bitcast(F32).rearrange("(u q) -> u q", q=P)
        )
        nc.sync.dma_start(out=x_tiles[2][:], in_=x_groups[2])
        nc.sync.dma_start(out=x_tiles[3][:], in_=x_groups[3])
        nc.sync.dma_start(out=bias[:].rearrange("p o f -> p (o f)"), in_=b_qkv.partition_broadcast(P))
        for s in range(4, N_GROUPS):
            nc.sync.dma_start(out=x_tiles[s][:], in_=x_groups[s])

        ident_f32 = consts.tile([P, P], F32)
        make_identity(nc, ident_f32[:])
        eps = consts.tile([P, 1], F32)
        nc.vector.memset(eps[:], LN_EPS)
        warm = consts.tile([P, 1], F32)
        nc.scalar.activation(out=warm[:], in_=eps[:], func=ACT.Sqrt)

        affine = consts.tile([P, 2 * PACK], F32)

        def turn_affine():
            affine_ps = turn_psum.tile([P, P], F32, tag="turn")
            nc.tensor.transpose(affine_ps[:], affine_rows[:], ident_f32[:])
            affine_words = consts.tile([P, 2 * HALVES], F32)
            nc.vector.tensor_copy(out=affine_words[:], in_=affine_ps[:, 0 : 2 * HALVES])
            nc.vector.tensor_copy(out=affine[:], in_=affine_words[:].bitcast(BF16))

        w_words = w_sb[:].bitcast(F32)
        w_grouped = consts.tile([P, OUTS * D, PACK], BF16, align_bytes=64)
        w_grouped_words = w_grouped[:].bitcast(F32)
        w_codes = consts.tile([P, OUTS * D], U32, align_bytes=64)
        w_scales = consts.tile([P, OUTS * D], U8, align_bytes=64)

        def turn_weight_tile(r):
            w_turned = acc_psum.tile([P, HALVES, P], F32, tag="acc_%d" % (r % OUTS))
            for u in range(HALVES):
                nc.tensor.transpose(w_turned[:, u, :], w_words[:, r, u * P : (u + 1) * P], ident_f32[:])
            dst = w_grouped_words[:, r * P : (r + 1) * P, :]
            src = w_turned[:].rearrange("p u f -> p f u")
            if r < PACK:
                nc.scalar.copy(out=dst, in_=src)
            else:
                nc.vector.tensor_copy(out=dst, in_=src)

        def quantise_weights(o):
            cols = slice(o * D, (o + 1) * D)
            nc.vector.quantize_mx(
                out=w_codes[:, cols].bitcast(FP8X4),
                scales=w_scales[:, cols],
                in_=w_grouped[:, cols, :].rearrange("p f t -> p (f t)"),
            )

        stats_of = {}
        mean_var_of = {}
        std_of = {}
        rstd_of = {}
        shift_of = {}
        xhat_of = {}
        turned_of = {}
        planes_of = {}
        grouped_of = {}
        codes_of = {}
        scales_of = {}
        accs_of = {}
        stage_of = {}

        def statistics(s, i):
            if i == 0:
                stats_of[s] = small.tile([P, ROWS, 6], F32, name="stats")
            nc.vector.bn_stats(out=stats_of[s][:, i, :], in_=x_tiles[s][:, i, :])

        def mean_and_std(s):
            mean_var = small.tile([P, ROWS, 2], F32)
            for i in range(ROWS):
                nc.vector.bn_aggr(out=mean_var[:, i, :], in_=stats_of[s][:, i, :])
            std = small.tile([P, ROWS], F32)
            nc.scalar.activation(out=std[:], in_=mean_var[:, :, 1], func=ACT.Sqrt, bias=eps[:, 0:1], scale=1.0)
            mean_var_of[s] = mean_var
            std_of[s] = std

        def reciprocal_std(s):
            rstd_of[s] = small.tile([P, ROWS], F32, name="rstd")
            nc.vector.reciprocal(out=rstd_of[s][:], in_=std_of[s][:])

        def shift(s):
            shift_of[s] = small.tile([P, ROWS], F32, name="shift")
            nc.vector.scalar_tensor_tensor(
                out=shift_of[s][:],
                in0=mean_var_of[s][:, :, 0],
                scalar=-1.0,
                in1=rstd_of[s][:],
                op0=ALU.mult,
                op1=ALU.mult,
            )

        def normalise_row(s, i):
            if i == 0:
                xhat_of[s] = xhat_pool.tile([P, ROWS, D], F32, name="xhat")
            dst = xhat_of[s][:, i, :].rearrange("p (u e q) -> p u e q", u=HALVES, e=2)
            src = x_tiles[s][:, i, :].rearrange("p (u q e) -> p u e q", u=HALVES, e=2)
            if i == 0:
                nc.scalar.activation(
                    out=dst,
                    in_=src,
                    func=ACT.Identity,
                    scale=rstd_of[s][:, i : i + 1],
                    bias=shift_of[s][:, i : i + 1],
                )
            else:
                nc.gpsimd.tensor_scalar(
                    out=dst,
                    in0=src,
                    scalar1=rstd_of[s][:, i : i + 1],
                    scalar2=shift_of[s][:, i : i + 1],
                    op0=ALU.mult,
                    op1=ALU.add,
                )

        def turn_plane(s, t):
            plane = turn_psum.tile([P, GROUP], F32, tag="turn")
            for i in range(ROWS):
                nc.tensor.transpose(
                    plane[:, i * P : (i + 1) * P], xhat_of[s][:, i, t * P : (t + 1) * P], ident_f32[:]
                )
            turned_of[s, t] = plane

        def plane_out(s, t):
            if t == 0:
                planes_of[s] = plane_pool.tile([P, PACK, GROUP], BF16, name="planes")
            nc.scalar.activation(
                out=planes_of[s][:, t, :],
                in_=turned_of[s, t][:],
                func=ACT.Identity,
                scale=affine[:, t : t + 1],
                bias=affine[:, PACK + t : PACK + t + 1],
            )

        def regroup_row(s, i):
            grouped = row_pool.tile([P, P, PACK], BF16, align_bytes=64)
            nc.scalar.copy(
                out=grouped[:].rearrange("p (c j) t -> p c t j", j=4),
                in_=planes_of[s][:, :, i * P : (i + 1) * P].rearrange("p t (c j) -> p c t j", j=4),
            )
            grouped_of[s, i] = grouped

        def quantise_row(s, i):
            codes = row_pool.tile([P, P], U32, align_bytes=64)
            scales = row_pool.tile([P, P], U8, align_bytes=64)
            nc.vector.quantize_mx(
                out=codes[:].bitcast(FP8X4),
                scales=scales[:],
                in_=grouped_of[s, i][:].rearrange("p c t -> p (c t)"),
            )
            codes_of[s, i] = codes
            scales_of[s, i] = scales

        def matmul_row(s, i):
            accs = []
            for o in range(OUTS):
                acc = acc_psum.tile([P, D], F32, name="acc_%d" % o)
                nc.tensor.matmul_mx(
                    out=acc[:],
                    lhsT=codes_of[s, i][:].bitcast(FP8X4),
                    lhsT_scale=scales_of[s, i][:],
                    rhs=w_codes[:, o * D : (o + 1) * D].bitcast(FP8X4),
                    rhs_scale=w_scales[:, o * D : (o + 1) * D],
                    start=True,
                    stop=True,
                )
                accs.append(acc)
            accs_of[s, i] = accs

        def bias_row(s, i):
            if i == 0:
                stage_of[s] = [
                    stage_pool.tile([P, ROWS, D], F32, name="stage_%d" % o) for o in range(OUTS)
                ]
            accs = accs_of[s, i]
            for o in range(OUTS):
                dst = stage_of[s][o][:, i, :]
                if o < OUTS - 1:
                    nc.vector.tensor_tensor(out=dst, in0=accs[o][:], in1=bias[:, o, :], op=ALU.add)
                else:
                    nc.scalar.copy(out=dst, in_=accs[o][:])
                    nc.gpsimd.tensor_tensor(out=dst, in0=dst, in1=bias[:, o, :], op=ALU.add)
            if (i + 1) % STORE_ROWS == 0:
                done = slice(i + 1 - STORE_ROWS, i + 1)
                for o in range(OUTS):
                    nc.sync.dma_start(out=out_groups[o][s][:, done, :], in_=stage_of[s][o][:, done, :])

        for step in range(N_STEPS):
            n = step - LAG_RSTD
            group_is_counted = n % ROWS == 0 and 0 <= n < N_ROWS
            if group_is_counted:
                mean_and_std(n // ROWS)
            if step < N_ROWS:
                statistics(step // ROWS, step % ROWS)
            if group_is_counted:
                reciprocal_std(n // ROWS)
            n = step - LAG_XHAT
            if 0 <= n < N_ROWS:
                normalise_row(n // ROWS, n % ROWS)
            if step < W_TILES:
                turn_weight_tile(step)
            elif step < W_TILES + OUTS:
                quantise_weights(step - W_TILES)
            if step == LAG_TURN - 1:
                turn_affine()
            n = step - LAG_TURN
            if 0 <= n < N_ROWS:
                turn_plane(n // PACK, n % PACK)
            n = step - LAG_PLANE_OUT
            if 0 <= n < N_ROWS:
                plane_out(n // PACK, n % PACK)
            n = step - LAG_MATMUL
            if 0 <= n < N_ROWS:
                matmul_row(n // ROWS, n % ROWS)
            n = step - LAG_BIAS
            if 0 <= n < N_ROWS:
                bias_row(n // ROWS, n % ROWS)
            if group_is_counted:
                shift((step - LAG_RSTD) // ROWS)
            n = step - LAG_REGROUP
            if 0 <= n < N_ROWS:
                regroup_row(n // ROWS, n % ROWS)
            n = step - LAG_QUANTISE
            if 0 <= n < N_ROWS:
                quantise_row(n // ROWS, n % ROWS)
